import numpy as np
import ml_dtypes


def mxq(x, axis, fmt="e4m3"):
    dtype, down = {"e4m3": (ml_dtypes.float8_e4m3fn, 7), "e5m2": (ml_dtypes.float8_e5m2, 14)}[fmt]
    v = np.moveaxis(np.asarray(x, np.float32).astype(ml_dtypes.bfloat16).astype(np.float64), axis, -1)
    blocks = v.reshape(v.shape[:-1] + (-1, 32))
    amax = np.abs(blocks).max(-1, keepdims=True)
    byte = np.maximum(np.where(amax > 0, np.frexp(amax)[1] - 1 + 127, 0) - down, 1)
    scale = np.exp2(byte - 127.0)
    codes = (blocks / scale).astype(np.float32).astype(dtype).astype(np.float64)
    return np.moveaxis((codes * scale).reshape(v.shape), -1, axis)


WIDE = False


def mx_kscale(k):
    if not WIDE:
        return np.ones(k)
    levels = np.array([10, -10, 5, -5, 0])
    a = np.random.permutation(np.resize(levels, k // 512 * 4)).reshape(k // 512, 4)
    idx = np.arange(k)
    return np.exp2(a[idx // 512, idx % 128 // 32])


BF16 = ml_dtypes.bfloat16


def bf(x):
    return np.asarray(x, np.float32).astype(BF16)


def f64(x):
    return np.asarray(x).astype(np.float64)


B, A, E, P, R = 256, 8, 512, 512, 512


def setup_inputs():
    s = mx_kscale(R)
    return {
        "attr_rep": bf(np.random.standard_normal((B, A, R)) * s),
        "bwd_proj": bf(np.random.standard_normal((A, R, P)) / np.sqrt(R) / s[:, None]),
        "self_weighted": bf(1.0 + 0.3 * np.random.standard_normal((1, A, 1))),
    }


def reference(attr_rep, bwd_proj, self_weighted):
    proj = (mxq(f64(attr_rep).transpose(1, 0, 2), 2, "e4m3") @ mxq(f64(bwd_proj), 1, "e4m3")).transpose(1, 0, 2)
    return np.sum(np.maximum(proj, 0.0) * f64(self_weighted), axis=1)

@@ -1,0 +1,118 @@
+from contextlib import ExitStack
+
+import concourse.bass as bass
+import concourse.mybir as mybir
+import concourse.tile as tile
+from concourse.masks import make_identity
+
+F32 = mybir.dt.float32
+BF16 = mybir.dt.bfloat16
+U32 = mybir.dt.uint32
+U8 = mybir.dt.uint8
+FP8X4 = mybir.dt.float8_e4m3fn_x4
+ALU = mybir.AluOpType
+ACT = mybir.ActivationFunctionType
+
+P = 128
+NB = 256
+BT = 2
+A = 8
+R = 512
+C = 512
+FLOPS = 2 * NB * A * R * C
+
+V_COLS = 256
+
+
+def tile_attributegnn_pb_kernel(tc, attr_rep, bwd_proj, self_weighted, out):
+    nc = tc.nc
+    with ExitStack() as ctx:
+        keep = ctx.enter_context(tc.tile_pool(name="keep", bufs=1))
+        work = ctx.enter_context(tc.tile_pool(name="work", bufs=3))
+        relu_pool = ctx.enter_context(tc.tile_pool(name="relu", bufs=4))
+        ps_x = ctx.enter_context(tc.psum_pool(name="psx", bufs=2))
+        ps_m = ctx.enter_context(tc.psum_pool(name="psm", bufs=4))
+
+        w_bf = keep.tile([P, A], BF16, name="w_bf")
+        nc.scalar.dma_start(out=w_bf[:], in_=self_weighted.rearrange("o a i -> (o a i)").partition_broadcast(P))
+        ident = keep.tile([P, P], F32, name="ident")
+        make_identity(nc, ident[:])
+
+        x_sb = keep.tile([P, BT * A * R], BF16, name="x_sb")
+        x_dst = x_sb[:].rearrange("p (t a k) -> p t a k", t=BT, a=A)
+        x_src = attr_rep.rearrange("(t p) a k -> p t a k", p=P)
+        w_raw = []
+        for a in range(A):
+            w_raw.append(keep.tile([P, 4, C], BF16, name="w_raw%d" % a))
+
+        def load_w(a):
+            nc.sync.dma_start(out=w_raw[a][:], in_=bwd_proj[a].rearrange("(p j) c -> p j c", j=4))
+
+        def load_x(a0):
+            nc.sync.dma_start(out=x_dst[:, :, a0:a0 + 2, :], in_=x_src[:, :, a0:a0 + 2, :])
+
+        for a0 in range(0, A, 2):
+            load_w(a0)
+            load_x(a0)
+            load_w(a0 + 1)
+
+        w32 = keep.tile([P, A], F32, name="w32")
+        nc.vector.tensor_copy(out=w32[:], in_=w_bf[:])
+
+        x_words = x_sb[:].bitcast(F32)
+
+        xc = keep.tile([P, A * NB], U32, name="xc", align_bytes=64)
+        xs = keep.tile([P, A * NB], U8, name="xs", align_bytes=64)
+        wc = keep.tile([P, A * C], U32, name="wc", align_bytes=64)
+        ws = keep.tile([P, A * C], U8, name="ws", align_bytes=64)
+        acc = []
+        for bt in range(BT):
+            acc.append(keep.tile([P, C], F32, name="acc%d" % bt))
+
+        def prepare(a):
+            xt = ps_x.tile([P, 2, NB], F32, name="xt")
+            for bt in range(BT):
+                for u in range(2):
+                    s = (bt * A + a) * (R // 2) + u
+                    nc.tensor.transpose(xt[:, u, bt * P:(bt + 1) * P], x_words[:, s:s + R // 2 - 1:2], ident[:])
+            xg = work.tile([P, NB * 4], BF16, name="xg", align_bytes=64)
+            nc.scalar.copy(
+                out=xg[:].bitcast(F32).rearrange("p (c u) -> p c u", u=2),
+                in_=xt[:].rearrange("p u c -> p c u"),
+            )
+            wg = work.tile([P, C * 4], BF16, name="wg", align_bytes=64)
+            dst = wg[:].rearrange("p (c i t) -> p c t i", i=4, t=4)
+            src = w_raw[a][:].rearrange("p t (c i) -> p c t i", i=4)
+            cv = V_COLS // 4
+            nc.vector.tensor_copy(out=dst[:, 0:cv], in_=src[:, 0:cv])
+            nc.scalar.copy(out=dst[:, cv:], in_=src[:, cv:])
+            nc.vector.quantize_mx(
+                out=xc[:, a * NB:(a + 1) * NB].bitcast(FP8X4), scales=xs[:, a * NB:(a + 1) * NB], in_=xg[:])
+            nc.vector.quantize_mx(
+                out=wc[:, a * C:(a + 1) * C].bitcast(FP8X4), scales=ws[:, a * C:(a + 1) * C], in_=wg[:])
+
+        def multiply(a):
+            for bt in range(BT):
+                pm = ps_m.tile([P, C], F32, name="pm")
+                lo = a * NB + bt * P
+                nc.tensor.matmul_mx(
+                    out=pm[:],
+                    lhsT=xc[:, lo:lo + P].bitcast(FP8X4), lhsT_scale=xs[:, lo:lo + P],
+                    rhs=wc[:, a * C:(a + 1) * C].bitcast(FP8X4), rhs_scale=ws[:, a * C:(a + 1) * C],
+                    start=True, stop=True)
+                if a == 0:
+                    nc.vector.tensor_scalar(out=acc[bt][:], in0=pm[:], scalar1=0.0, scalar2=w32[:, 0:1],
+                                            op0=ALU.max, op1=ALU.mult)
+                else:
+                    rl = relu_pool.tile([P, C], F32, name="rl")
+                    nc.scalar.activation(out=rl[:], in_=pm[:], func=ACT.Relu)
+                    nc.vector.scalar_tensor_tensor(out=acc[bt][:], in0=rl[:], scalar=w32[:, a:a + 1], in1=acc[bt][:],
+                                                   op0=ALU.mult, op1=ALU.add)
+                if a == A - 1:
+                    nc.sync.dma_start(out=out[bt * P:(bt + 1) * P, :], in_=acc[bt][:])
+
+        prepare(0)
+        for a in range(1, A):
+            prepare(a)
+            multiply(a - 1)
+        multiply(A - 1)

@@ -1,8 +1,6 @@
 from contextlib import ExitStack
 
-import concourse.bass as bass
 import concourse.mybir as mybir
-import concourse.tile as tile
 from concourse.masks import make_identity
 
 F32 = mybir.dt.float32
@@ -19,19 +17,20 @@ BT = 2
 A = 8
 R = 512
 C = 512
+H = 2
+HC = C // H
 FLOPS = 2 * NB * A * R * C
 
-V_COLS = 256
+V_UNITS = ((0, 0), (1, 0), (3, 0), (5, 0))
+S_BANKS = ((6, 1), (7, 1))
 
 
 def tile_attributegnn_pb_kernel(tc, attr_rep, bwd_proj, self_weighted, out):
     nc = tc.nc
     with ExitStack() as ctx:
         keep = ctx.enter_context(tc.tile_pool(name="keep", bufs=1))
-        work = ctx.enter_context(tc.tile_pool(name="work", bufs=3))
-        relu_pool = ctx.enter_context(tc.tile_pool(name="relu", bufs=4))
-        ps_x = ctx.enter_context(tc.psum_pool(name="psx", bufs=2))
-        ps_m = ctx.enter_context(tc.psum_pool(name="psm", bufs=4))
+        psum = ctx.enter_context(tc.psum_pool(name="psum", bufs=1))
+        ctx.enter_context(tc.manual_schedule())
 
         w_bf = keep.tile([P, A], BF16, name="w_bf")
         nc.scalar.dma_start(out=w_bf[:], in_=self_weighted.rearrange("o a i -> (o a i)").partition_broadcast(P))
@@ -46,19 +45,18 @@ def tile_attributegnn_pb_kernel(tc, attr_rep, bwd_proj, self_weighted, out):
             w_raw.append(keep.tile([P, 4, C], BF16, name="w_raw%d" % a))
 
         def load_w(a):
-            nc.sync.dma_start(out=w_raw[a][:], in_=bwd_proj[a].rearrange("(p j) c -> p j c", j=4))
+            nc.sync.dma_start(out=w_raw[a][:].rearrange("p (u e) c -> p u (e c)", u=2),
+                              in_=bwd_proj[a].rearrange("(u p e) c -> p u (e c)", u=2, e=2))
 
         def load_x(a0):
             nc.sync.dma_start(out=x_dst[:, :, a0:a0 + 2, :], in_=x_src[:, :, a0:a0 + 2, :])
 
         for a0 in range(0, A, 2):
-            load_w(a0)
             load_x(a0)
+            load_w(a0)
             load_w(a0 + 1)
 
         w32 = keep.tile([P, A], F32, name="w32")
-        nc.vector.tensor_copy(out=w32[:], in_=w_bf[:])
-
         x_words = x_sb[:].bitcast(F32)
 
         xc = keep.tile([P, A * NB], U32, name="xc", align_bytes=64)
@@ -66,53 +64,106 @@ def tile_attributegnn_pb_kernel(tc, attr_rep, bwd_proj, self_weighted, out):
         wc = keep.tile([P, A * C], U32, name="wc", align_bytes=64)
         ws = keep.tile([P, A * C], U8, name="ws", align_bytes=64)
         acc = []
-        for bt in range(BT):
-            acc.append(keep.tile([P, C], F32, name="acc%d" % bt))
+        for h in range(H):
+            acc.append(psum.tile([P, BT, HC], F32, name="acc%d" % h))
+        xt = {}
+        xg = {}
+        wg = {}
+        pm = {}
+        rl = {}
 
-        def prepare(a):
-            xt = ps_x.tile([P, 2, NB], F32, name="xt")
+        def tx(a):
+            xt[a] = psum.tile([P, 2, NB], F32, name="xt%d" % (a % 2))
             for bt in range(BT):
                 for u in range(2):
-                    s = (bt * A + a) * (R // 2) + u
-                    nc.tensor.transpose(xt[:, u, bt * P:(bt + 1) * P], x_words[:, s:s + R // 2 - 1:2], ident[:])
-            xg = work.tile([P, NB * 4], BF16, name="xg", align_bytes=64)
-            nc.scalar.copy(
-                out=xg[:].bitcast(F32).rearrange("p (c u) -> p c u", u=2),
-                in_=xt[:].rearrange("p u c -> p c u"),
-            )
-            wg = work.tile([P, C * 4], BF16, name="wg", align_bytes=64)
-            dst = wg[:].rearrange("p (c i t) -> p c t i", i=4, t=4)
-            src = w_raw[a][:].rearrange("p t (c i) -> p c t i", i=4)
-            cv = V_COLS // 4
-            nc.vector.tensor_copy(out=dst[:, 0:cv], in_=src[:, 0:cv])
-            nc.scalar.copy(out=dst[:, cv:], in_=src[:, cv:])
-            nc.vector.quantize_mx(
-                out=xc[:, a * NB:(a + 1) * NB].bitcast(FP8X4), scales=xs[:, a * NB:(a + 1) * NB], in_=xg[:])
-            nc.vector.quantize_mx(
-                out=wc[:, a * C:(a + 1) * C].bitcast(FP8X4), scales=ws[:, a * C:(a + 1) * C], in_=wg[:])
+                    s = (bt * A + a) * (R // 2) + u * P
+                    nc.tensor.transpose(xt[a][:, u, bt * P:(bt + 1) * P], x_words[:, s:s + P], ident[:])
 
-        def multiply(a):
-            for bt in range(BT):
-                pm = ps_m.tile([P, C], F32, name="pm")
-                lo = a * NB + bt * P
+        def ex(a):
+            xg[a] = keep.tile([P, NB * 4], BF16, name="xg%d" % a, align_bytes=64)
+            nc.scalar.copy(out=xg[a][:].bitcast(F32).rearrange("p (c u) -> p c u", u=2),
+                           in_=xt[a][:].rearrange("p u c -> p c u"))
+
+        def regroup(a, h):
+            wg[a, h] = keep.tile([P, HC * 4], BF16, name="wg%d_%d" % (a, h), align_bytes=64)
+            dst = wg[a, h][:].rearrange("p (c i t) -> p c t i", i=4, t=4)
+            src = w_raw[a][:, :, h * HC:(h + 1) * HC].rearrange("p t (c i) -> p c t i", i=4)
+            if (a, h) in V_UNITS:
+                nc.vector.tensor_copy(out=dst, in_=src)
+            else:
+                nc.scalar.copy(out=dst, in_=src)
+
+        def qx(a):
+            nc.vector.quantize_mx(out=xc[:, a * NB:(a + 1) * NB].bitcast(FP8X4), scales=xs[:, a * NB:(a + 1) * NB],
+                                  in_=xg[a][:])
+
+        def qw(a, h):
+            lo = a * C + h * HC
+            nc.vector.quantize_mx(out=wc[:, lo:lo + HC].bitcast(FP8X4), scales=ws[:, lo:lo + HC], in_=wg[a, h][:])
+
+        def mm(a, h):
+            pm[a, h] = psum.tile([P, 2, NB], F32, name="pm%d" % ((2 * a + h) % 4))
+            for jj in range(2):
+                lo = a * C + h * HC + jj * P
                 nc.tensor.matmul_mx(
-                    out=pm[:],
-                    lhsT=xc[:, lo:lo + P].bitcast(FP8X4), lhsT_scale=xs[:, lo:lo + P],
-                    rhs=wc[:, a * C:(a + 1) * C].bitcast(FP8X4), rhs_scale=ws[:, a * C:(a + 1) * C],
+                    out=pm[a, h][:, jj, :],
+                    lhsT=wc[:, lo:lo + P].bitcast(FP8X4), lhsT_scale=ws[:, lo:lo + P],
+                    rhs=xc[:, a * NB:(a + 1) * NB].bitcast(FP8X4), rhs_scale=xs[:, a * NB:(a + 1) * NB],
                     start=True, stop=True)
-                if a == 0:
-                    nc.vector.tensor_scalar(out=acc[bt][:], in0=pm[:], scalar1=0.0, scalar2=w32[:, 0:1],
-                                            op0=ALU.max, op1=ALU.mult)
-                else:
-                    rl = relu_pool.tile([P, C], F32, name="rl")
-                    nc.scalar.activation(out=rl[:], in_=pm[:], func=ACT.Relu)
-                    nc.vector.scalar_tensor_tensor(out=acc[bt][:], in0=rl[:], scalar=w32[:, a:a + 1], in1=acc[bt][:],
-                                                   op0=ALU.mult, op1=ALU.add)
-                if a == A - 1:
-                    nc.sync.dma_start(out=out[bt * P:(bt + 1) * P, :], in_=acc[bt][:])
 
-        prepare(0)
-        for a in range(1, A):
-            prepare(a)
-            multiply(a - 1)
-        multiply(A - 1)
+        def s1(a, h):
+            rl[a, h] = keep.tile([P, 2 * NB], F32, name="rl%d" % ((2 * a + h) % 4))
+            prod = pm[a, h][:].rearrange("p j b -> p (j b)")
+            if (a, h) in S_BANKS:
+                rr = keep.tile([P, 2 * NB], F32, name="rr%d" % (a % 2))
+                nc.scalar.activation(out=rr[:], in_=prod, func=ACT.Relu)
+                nc.scalar.activation(out=rl[a, h][:], in_=rr[:], func=ACT.Copy, scale=w32[:, a:a + 1])
+            else:
+                nc.vector.tensor_scalar(out=rl[a, h][:], in0=prod, scalar1=0.0, scalar2=w32[:, a:a + 1],
+                                        op0=ALU.max, op1=ALU.mult)
+
+        def ta(a, h):
+            for jj in range(2):
+                for bt in range(BT):
+                    nc.tensor.matmul(
+                        out=acc[h][:, bt, jj * P:(jj + 1) * P],
+                        lhsT=rl[a, h][:, jj * NB + bt * P:jj * NB + (bt + 1) * P], rhs=ident[:],
+                        is_transpose=True,
+                        start=(a == 0 and jj == 0 and bt == 0), stop=(a == A - 1 and jj == 1 and bt == BT - 1))
+
+        out_v = out.rearrange("(t p) c -> p t c", p=P)
+
+        def finish(h):
+            res = keep.tile([P, BT, HC], F32, name="res%d" % h)
+            if h == 0:
+                nc.scalar.copy(out=res[:], in_=acc[h][:])
+            else:
+                nc.vector.tensor_copy(out=res[:], in_=acc[h][:])
+            nc.sync.dma_start(out=out_v[:, :, h * HC:(h + 1) * HC], in_=res[:])
+
+        tx(0)
+        for i in range(A + 2):
+            if i + 1 < A:
+                tx(i + 1)
+            if i < A:
+                if i == 0:
+                    ex(0)
+                regroup(i, 0)
+                regroup(i, 1)
+                if i + 1 < A:
+                    ex(i + 1)
+            b = i - 1
+            if 0 <= b < A:
+                qx(b)
+                for h in range(H):
+                    qw(b, h)
+                    mm(b, h)
+            c = i - 2
+            if c == 0:
+                nc.vector.tensor_copy(out=w32[:], in_=w_bf[:])
+            if 0 <= c < A:
+                for h in range(H):
+                    s1(c, h)
+                    ta(c, h)
+                    if c == A - 1:
+                        finish(h)

@@ -37,9 +37,10 @@ def tile_attributegnn_pb_kernel(tc, attr_rep, bwd_proj, self_weighted, out):
         ident = keep.tile([P, P], F32, name="ident")
         make_identity(nc, ident[:])
 
-        x_sb = keep.tile([P, BT * A * R], BF16, name="x_sb")
-        x_dst = x_sb[:].rearrange("p (t a k) -> p t a k", t=BT, a=A)
         x_src = attr_rep.rearrange("(t p) a k -> p t a k", p=P)
+        x_sb = []
+        for g in range(A // 2):
+            x_sb.append(keep.tile([P, BT * 2 * R], BF16, name="x_sb%d" % g))
         w_raw = []
         for a in range(A):
             w_raw.append(keep.tile([P, 4, C], BF16, name="w_raw%d" % a))
@@ -49,7 +50,8 @@ def tile_attributegnn_pb_kernel(tc, attr_rep, bwd_proj, self_weighted, out):
                               in_=bwd_proj[a].rearrange("(u p e) c -> p u (e c)", u=2, e=2))
 
         def load_x(a0):
-            nc.sync.dma_start(out=x_dst[:, :, a0:a0 + 2, :], in_=x_src[:, :, a0:a0 + 2, :])
+            nc.sync.dma_start(out=x_sb[a0 // 2][:].rearrange("p (t q) -> p t q", t=BT),
+                              in_=x_src[:, :, a0:a0 + 2, :].rearrange("p t a k -> p t (a k)"))
 
         for a0 in range(0, A, 2):
             load_x(a0)
@@ -57,7 +59,6 @@ def tile_attributegnn_pb_kernel(tc, attr_rep, bwd_proj, self_weighted, out):
             load_w(a0 + 1)
 
         w32 = keep.tile([P, A], F32, name="w32")
-        x_words = x_sb[:].bitcast(F32)
 
         xc = keep.tile([P, A * NB], U32, name="xc", align_bytes=64)
         xs = keep.tile([P, A * NB], U8, name="xs", align_bytes=64)
@@ -76,8 +77,9 @@ def tile_attributegnn_pb_kernel(tc, attr_rep, bwd_proj, self_weighted, out):
             xt[a] = psum.tile([P, 2, NB], F32, name="xt%d" % (a % 2))
             for bt in range(BT):
                 for u in range(2):
-                    s = (bt * A + a) * (R // 2) + u * P
-                    nc.tensor.transpose(xt[a][:, u, bt * P:(bt + 1) * P], x_words[:, s:s + P], ident[:])
+                    s = (bt * 2 + a % 2) * (R // 2) + u * P
+                    nc.tensor.transpose(xt[a][:, u, bt * P:(bt + 1) * P], x_sb[a // 2][:].bitcast(F32)[:, s:s + P],
+                                        ident[:])
 
         def ex(a):
             xg[a] = keep.tile([P, NB * 4], BF16, name="xg%d" % a, align_bytes=64)
@@ -165,5 +167,5 @@ def tile_attributegnn_pb_kernel(tc, attr_rep, bwd_proj, self_weighted, out):
                 for h in range(H):
                     s1(c, h)
                     ta(c, h)
-                    if c == A - 1:
-                        finish(h)
+        for h in range(H):
+            finish(h)

@@ -21,8 +21,10 @@ H = 2
 HC = C // H
 FLOPS = 2 * NB * A * R * C
 
-V_UNITS = ((0, 0), (1, 0), (3, 0), (5, 0))
-S_BANKS = ((6, 1), (7, 1))
+V_UNITS = ((0, 0), (1, 0), (4, 0))
+S_BANKS = ((6, 0), (7, 1))
+
+G_SET = (2, 3, 4, 5, 6, 7)
 
 
 def tile_attributegnn_pb_kernel(tc, attr_rep, bwd_proj, self_weighted, out):
@@ -72,6 +74,7 @@ def tile_attributegnn_pb_kernel(tc, attr_rep, bwd_proj, self_weighted, out):
         wg = {}
         pm = {}
         rl = {}
+        gg = {}
 
         def tx(a):
             xt[a] = psum.tile([P, 2, NB], F32, name="xt%d" % (a % 2))
@@ -87,9 +90,10 @@ def tile_attributegnn_pb_kernel(tc, attr_rep, bwd_proj, self_weighted, out):
                            in_=xt[a][:].rearrange("p u c -> p c u"))
 
         def regroup(a, h):
-            wg[a, h] = keep.tile([P, HC * 4], BF16, name="wg%d_%d" % (a, h), align_bytes=64)
+            cols = P if (h == 1 and a in G_SET) else HC
+            wg[a, h] = keep.tile([P, cols * 4], BF16, name="wg%d_%d" % (a, h), align_bytes=64)
             dst = wg[a, h][:].rearrange("p (c i t) -> p c t i", i=4, t=4)
-            src = w_raw[a][:, :, h * HC:(h + 1) * HC].rearrange("p t (c i) -> p c t i", i=4)
+            src = w_raw[a][:, :, h * HC:h * HC + cols].rearrange("p t (c i) -> p c t i", i=4)
             if (a, h) in V_UNITS:
                 nc.vector.tensor_copy(out=dst, in_=src)
             else:
@@ -99,9 +103,20 @@ def tile_attributegnn_pb_kernel(tc, attr_rep, bwd_proj, self_weighted, out):
             nc.vector.quantize_mx(out=xc[:, a * NB:(a + 1) * NB].bitcast(FP8X4), scales=xs[:, a * NB:(a + 1) * NB],
                                   in_=xg[a][:])
 
+        def regroup_g(a):
+            gg[a] = keep.tile([P, P * 4], BF16, name="gg", align_bytes=64)
+            nc.gpsimd.tensor_scalar(out=gg[a][:].rearrange("p (c t) -> p c t", t=4),
+                                    in0=w_raw[a][:, :, C - P:C].rearrange("p t c -> p c t"),
+                                    scalar1=1.0, scalar2=0.0, op0=ALU.mult, op1=ALU.add)
+
         def qw(a, h):
             lo = a * C + h * HC
-            nc.vector.quantize_mx(out=wc[:, lo:lo + HC].bitcast(FP8X4), scales=ws[:, lo:lo + HC], in_=wg[a, h][:])
+            if h == 1 and a in G_SET:
+                nc.vector.quantize_mx(out=wc[:, lo:lo + P].bitcast(FP8X4), scales=ws[:, lo:lo + P], in_=wg[a, h][:])
+                lo = lo + P
+                nc.vector.quantize_mx(out=wc[:, lo:lo + P].bitcast(FP8X4), scales=ws[:, lo:lo + P], in_=gg[a][:])
+            else:
+                nc.vector.quantize_mx(out=wc[:, lo:lo + HC].bitcast(FP8X4), scales=ws[:, lo:lo + HC], in_=wg[a, h][:])
 
         def mm(a, h):
             pm[a, h] = psum.tile([P, 2, NB], F32, name="pm%d" % ((2 * a + h) % 4))
@@ -160,6 +175,8 @@ def tile_attributegnn_pb_kernel(tc, attr_rep, bwd_proj, self_weighted, out):
                 for h in range(H):
                     qw(b, h)
                     mm(b, h)
+            if i in G_SET:
+                regroup_g(i)
             c = i - 2
             if c == 0:
                 nc.vector.tensor_copy(out=w32[:], in_=w_bf[:])

@@ -34,8 +34,11 @@ def tile_attributegnn_pb_kernel(tc, attr_rep, bwd_proj, self_weighted, out):
         psum = ctx.enter_context(tc.psum_pool(name="psum", bufs=1))
         ctx.enter_context(tc.manual_schedule())
 
-        w_bf = keep.tile([P, A], BF16, name="w_bf")
-        nc.scalar.dma_start(out=w_bf[:], in_=self_weighted.rearrange("o a i -> (o a i)").partition_broadcast(P))
+        w_row = keep.tile([P, 32], BF16, name="w_row")
+        nc.vector.memset(w_row[:], 0.0)
+        nc.scalar.dma_start(out=w_row[0:1, 0:A], in_=self_weighted.rearrange("o a i -> o (a i)"))
+        ones = keep.tile([P, P], BF16, name="ones")
+        nc.vector.memset(ones[:], 1.0)
         ident = keep.tile([P, P], F32, name="ident")
         make_identity(nc, ident[:])
 
@@ -158,6 +161,9 @@ def tile_attributegnn_pb_kernel(tc, attr_rep, bwd_proj, self_weighted, out):
                 nc.vector.tensor_copy(out=res[:], in_=acc[h][:])
             nc.sync.dma_start(out=out_v[:, :, h * HC:(h + 1) * HC], in_=res[:])
 
+        w_ps = psum.tile([P, 32], F32, name="pm3")
+        nc.tensor.matmul(out=w_ps[:], lhsT=ones[:], rhs=w_row[:], start=True, stop=True)
+        nc.vector.tensor_copy(out=w32[:], in_=w_ps[:, 0:A])
         tx(0)
         for i in range(A + 2):
             if i + 1 < A:
@@ -178,8 +184,6 @@ def tile_attributegnn_pb_kernel(tc, attr_rep, bwd_proj, self_weighted, out):
             if i in G_SET:
                 regroup_g(i)
             c = i - 2
-            if c == 0:
-                nc.vector.tensor_copy(out=w32[:], in_=w_bf[:])
             if 0 <= c < A:
                 for h in range(H):
                     s1(c, h)

@@ -70,8 +70,6 @@ def tile_attributegnn_pb_kernel(tc, attr_rep, bwd_proj, self_weighted, out):
         wc = keep.tile([P, A * C], U32, name="wc", align_bytes=64)
         ws = keep.tile([P, A * C], U8, name="ws", align_bytes=64)
         acc = []
-        for h in range(H):
-            acc.append(psum.tile([P, BT, HC], F32, name="acc%d" % h))
         xt = {}
         xg = {}
         wg = {}
@@ -161,9 +159,6 @@ def tile_attributegnn_pb_kernel(tc, attr_rep, bwd_proj, self_weighted, out):
                 nc.vector.tensor_copy(out=res[:], in_=acc[h][:])
             nc.sync.dma_start(out=out_v[:, :, h * HC:(h + 1) * HC], in_=res[:])
 
-        w_ps = psum.tile([P, 32], F32, name="pm3")
-        nc.tensor.matmul(out=w_ps[:], lhsT=ones[:], rhs=w_row[:], start=True, stop=True)
-        nc.vector.tensor_copy(out=w32[:], in_=w_ps[:, 0:A])
         tx(0)
         for i in range(A + 2):
             if i + 1 < A:
@@ -183,7 +178,14 @@ def tile_attributegnn_pb_kernel(tc, attr_rep, bwd_proj, self_weighted, out):
                     mm(b, h)
             if i in G_SET:
                 regroup_g(i)
+            if i == 0:
+                w_ps = psum.tile([P, 32], F32, name="acc0")
+                nc.tensor.matmul(out=w_ps[:], lhsT=ones[:], rhs=w_row[:], start=True, stop=True)
             c = i - 2
+            if c == 0:
+                nc.vector.tensor_copy(out=w32[:], in_=w_ps[:, 0:A])
+                for h in range(H):
+                    acc.append(psum.tile([P, BT, HC], F32, name="acc%d" % h))
             if 0 <= c < A:
                 for h in range(H):
                     s1(c, h)

@@ -22,7 +22,7 @@ HC = C // H
 FLOPS = 2 * NB * A * R * C
 
 V_UNITS = ((0, 0), (1, 0), (4, 0))
-S_BANKS = ((6, 0), (7, 1))
+S_BANKS = ((6, 0), (6, 1))
 
 G_SET = (2, 3, 4, 5, 6, 7)
 
@@ -133,7 +133,7 @@ def tile_attributegnn_pb_kernel(tc, attr_rep, bwd_proj, self_weighted, out):
             rl[a, h] = keep.tile([P, 2 * NB], F32, name="rl%d" % ((2 * a + h) % 4))
             prod = pm[a, h][:].rearrange("p j b -> p (j b)")
             if (a, h) in S_BANKS:
-                rr = keep.tile([P, 2 * NB], F32, name="rr%d" % (a % 2))
+                rr = keep.tile([P, 2 * NB], F32, name="rr%d" % h)
                 nc.scalar.activation(out=rr[:], in_=prod, func=ACT.Relu)
                 nc.scalar.activation(out=rl[a, h][:], in_=rr[:], func=ACT.Copy, scale=w32[:, a:a + 1])
             else:
@@ -186,9 +186,13 @@ def tile_attributegnn_pb_kernel(tc, attr_rep, bwd_proj, self_weighted, out):
                 nc.vector.tensor_copy(out=w32[:], in_=w_ps[:, 0:A])
                 for h in range(H):
                     acc.append(psum.tile([P, BT, HC], F32, name="acc%d" % h))
-            if 0 <= c < A:
+            if 0 <= c < A - 2:
                 for h in range(H):
                     s1(c, h)
                     ta(c, h)
+        for h in range(H):
+            for c in (A - 2, A - 1):
+                s1(c, h)
+                ta(c, h)
         for h in range(H):
             finish(h)

@@ -22,7 +22,6 @@ HC = C // H
 FLOPS = 2 * NB * A * R * C
 
 V_UNITS = ((0, 0), (1, 0), (4, 0))
-S_BANKS = ((6, 0), (6, 1))
 
 G_SET = (2, 3, 4, 5, 6, 7)
 
@@ -113,9 +112,8 @@ def tile_attributegnn_pb_kernel(tc, attr_rep, bwd_proj, self_weighted, out):
         def qw(a, h):
             lo = a * C + h * HC
             if h == 1 and a in G_SET:
+                nc.vector.quantize_mx(out=wc[:, lo + P:lo + HC].bitcast(FP8X4), scales=ws[:, lo + P:lo + HC], in_=gg[a][:])
                 nc.vector.quantize_mx(out=wc[:, lo:lo + P].bitcast(FP8X4), scales=ws[:, lo:lo + P], in_=wg[a, h][:])
-                lo = lo + P
-                nc.vector.quantize_mx(out=wc[:, lo:lo + P].bitcast(FP8X4), scales=ws[:, lo:lo + P], in_=gg[a][:])
             else:
                 nc.vector.quantize_mx(out=wc[:, lo:lo + HC].bitcast(FP8X4), scales=ws[:, lo:lo + HC], in_=wg[a, h][:])
 
@@ -129,19 +127,21 @@ def tile_attributegnn_pb_kernel(tc, attr_rep, bwd_proj, self_weighted, out):
                     rhs=xc[:, a * NB:(a + 1) * NB].bitcast(FP8X4), rhs_scale=xs[:, a * NB:(a + 1) * NB],
                     start=True, stop=True)
 
-        def s1(a, h):
-            rl[a, h] = keep.tile([P, 2 * NB], F32, name="rl%d" % ((2 * a + h) % 4))
-            prod = pm[a, h][:].rearrange("p j b -> p (j b)")
-            if (a, h) in S_BANKS:
+        def s1(a, h, eng, jjs=(0, 1)):
+            if (a, h) not in rl:
+                rl[a, h] = keep.tile([P, 2 * NB], F32, name="rl%d" % ((2 * a + h) % 4))
+            lo, hi = jjs[0] * NB, (jjs[-1] + 1) * NB
+            prod = pm[a, h][:].rearrange("p j b -> p (j b)")[:, lo:hi]
+            if eng == "S":
                 rr = keep.tile([P, 2 * NB], F32, name="rr%d" % h)
-                nc.scalar.activation(out=rr[:], in_=prod, func=ACT.Relu)
-                nc.scalar.activation(out=rl[a, h][:], in_=rr[:], func=ACT.Copy, scale=w32[:, a:a + 1])
+                nc.scalar.activation(out=rr[:, lo:hi], in_=prod, func=ACT.Relu)
+                nc.scalar.activation(out=rl[a, h][:, lo:hi], in_=rr[:, lo:hi], func=ACT.Copy, scale=w32[:, a:a + 1])
             else:
-                nc.vector.tensor_scalar(out=rl[a, h][:], in0=prod, scalar1=0.0, scalar2=w32[:, a:a + 1],
+                nc.vector.tensor_scalar(out=rl[a, h][:, lo:hi], in0=prod, scalar1=0.0, scalar2=w32[:, a:a + 1],
                                         op0=ALU.max, op1=ALU.mult)
 
-        def ta(a, h):
-            for jj in range(2):
+        def ta(a, h, jjs=(0, 1)):
+            for jj in jjs:
                 for bt in range(BT):
                     nc.tensor.matmul(
                         out=acc[h][:, bt, jj * P:(jj + 1) * P],
@@ -151,13 +151,15 @@ def tile_attributegnn_pb_kernel(tc, attr_rep, bwd_proj, self_weighted, out):
 
         out_v = out.rearrange("(t p) c -> p t c", p=P)
 
-        def finish(h):
+        def finish(h, eng, bts):
             res = keep.tile([P, BT, HC], F32, name="res%d" % h)
-            if h == 0:
-                nc.scalar.copy(out=res[:], in_=acc[h][:])
-            else:
-                nc.vector.tensor_copy(out=res[:], in_=acc[h][:])
-            nc.sync.dma_start(out=out_v[:, :, h * HC:(h + 1) * HC], in_=res[:])
+            for bt in bts:
+                part = slice(bt, bt + 1) if len(bts) > 1 else slice(0, BT)
+                if eng == "S":
+                    nc.scalar.copy(out=res[:, part, :], in_=acc[h][:, part, :])
+                else:
+                    nc.vector.tensor_copy(out=res[:, part, :], in_=acc[h][:, part, :])
+                nc.sync.dma_start(out=out_v[:, part, h * HC:(h + 1) * HC], in_=res[:, part, :])
 
         tx(0)
         for i in range(A + 2):
@@ -188,11 +190,18 @@ def tile_attributegnn_pb_kernel(tc, attr_rep, bwd_proj, self_weighted, out):
                     acc.append(psum.tile([P, BT, HC], F32, name="acc%d" % h))
             if 0 <= c < A - 2:
                 for h in range(H):
-                    s1(c, h)
+                    s1(c, h, "V")
                     ta(c, h)
-        for h in range(H):
-            for c in (A - 2, A - 1):
-                s1(c, h)
-                ta(c, h)
-        for h in range(H):
-            finish(h)
+        s1(6, 0, "S")
+        ta(6, 0)
+        s1(6, 1, "V", (0,))
+        ta(6, 1, (0,))
+        s1(7, 0, "V")
+        ta(7, 0)
+        s1(6, 1, "S", (1,))
+        ta(6, 1, (1,))
+        for jj in range(2):
+            s1(7, 1, "V", (jj,))
+            ta(7, 1, (jj,))
+        finish(0, "S", (0,))
+        finish(1, "V", (0, 1))

@@ -92,8 +92,9 @@ def tile_attributegnn_pb_kernel(tc, attr_rep, bwd_proj, self_weighted, out):
         def regroup(a, h):
             cols = P if (h == 1 and a in G_SET) else HC
             wg[a, h] = keep.tile([P, cols * 4], BF16, name="wg%d_%d" % (a, h), align_bytes=64)
-            dst = wg[a, h][:].rearrange("p (c i t) -> p c t i", i=4, t=4)
-            src = w_raw[a][:, :, h * HC:h * HC + cols].rearrange("p t (c i) -> p c t i", i=4)
+            run = 4 if (a, h) in V_UNITS else 8
+            dst = wg[a, h][:].rearrange("p (c i t) -> p c t i", i=run, t=4)
+            src = w_raw[a][:, :, h * HC:h * HC + cols].rearrange("p t (c i) -> p c t i", i=run)
             if (a, h) in V_UNITS:
                 nc.vector.tensor_copy(out=dst, in_=src)
             else:

from contextlib import ExitStack

import concourse.mybir as mybir
from concourse.masks import make_identity

F32 = mybir.dt.float32
BF16 = mybir.dt.bfloat16
U32 = mybir.dt.uint32
U8 = mybir.dt.uint8
FP8X4 = mybir.dt.float8_e4m3fn_x4
ALU = mybir.AluOpType
ACT = mybir.ActivationFunctionType

P = 128
NB = 256
BT = 2
A = 8
R = 512
C = 512
H = 2
HC = C // H
FLOPS = 2 * NB * A * R * C

V_UNITS = ((0, 0), (1, 0), (4, 0))

G_SET = (2, 3, 4, 5, 6, 7)


def tile_attributegnn_pb_kernel(tc, attr_rep, bwd_proj, self_weighted, out):
    nc = tc.nc
    with ExitStack() as ctx:
        keep = ctx.enter_context(tc.tile_pool(name="keep", bufs=1))
        psum = ctx.enter_context(tc.psum_pool(name="psum", bufs=1))
        ctx.enter_context(tc.manual_schedule())

        w_row = keep.tile([P, 32], BF16, name="w_row")
        nc.vector.memset(w_row[:], 0.0)
        nc.scalar.dma_start(out=w_row[0:1, 0:A], in_=self_weighted.rearrange("o a i -> o (a i)"))
        ones = keep.tile([P, P], BF16, name="ones")
        nc.vector.memset(ones[:], 1.0)
        ident = keep.tile([P, P], F32, name="ident")
        make_identity(nc, ident[:])

        x_src = attr_rep.rearrange("(t p) a k -> p t a k", p=P)
        x_sb = []
        for g in range(A // 2):
            x_sb.append(keep.tile([P, BT * 2 * R], BF16, name="x_sb%d" % g))
        w_raw = []
        for a in range(A):
            w_raw.append(keep.tile([P, 4, C], BF16, name="w_raw%d" % a))

        def load_w(a):
            nc.sync.dma_start(out=w_raw[a][:].rearrange("p (u e) c -> p u (e c)", u=2),
                              in_=bwd_proj[a].rearrange("(u p e) c -> p u (e c)", u=2, e=2))

        def load_x(a0):
            nc.sync.dma_start(out=x_sb[a0 // 2][:].rearrange("p (t q) -> p t q", t=BT),
                              in_=x_src[:, :, a0:a0 + 2, :].rearrange("p t a k -> p t (a k)"))

        for a0 in range(0, A, 2):
            load_x(a0)
            load_w(a0)
            load_w(a0 + 1)

        w32 = keep.tile([P, A], F32, name="w32")

        xc = keep.tile([P, A * NB], U32, name="xc", align_bytes=64)
        xs = keep.tile([P, A * NB], U8, name="xs", align_bytes=64)
        wc = keep.tile([P, A * C], U32, name="wc", align_bytes=64)
        ws = keep.tile([P, A * C], U8, name="ws", align_bytes=64)
        acc = []
        xt = {}
        xg = {}
        wg = {}
        pm = {}
        rl = {}
        gg = {}

        def tx(a):
            xt[a] = psum.tile([P, 2, NB], F32, name="xt%d" % (a % 2))
            for bt in range(BT):
                for u in range(2):
                    s = (bt * 2 + a % 2) * (R // 2) + u * P
                    nc.tensor.transpose(xt[a][:, u, bt * P:(bt + 1) * P], x_sb[a // 2][:].bitcast(F32)[:, s:s + P],
                                        ident[:])

        def ex(a):
            xg[a] = keep.tile([P, NB * 4], BF16, name="xg%d" % a, align_bytes=64)
            nc.scalar.copy(out=xg[a][:].bitcast(F32).rearrange("p (c u) -> p c u", u=2),
                           in_=xt[a][:].rearrange("p u c -> p c u"))

        def regroup(a, h):
            cols = P if (h == 1 and a in G_SET) else HC
            wg[a, h] = keep.tile([P, cols * 4], BF16, name="wg%d_%d" % (a, h), align_bytes=64)
            run = 4 if (a, h) in V_UNITS else 8
            dst = wg[a, h][:].rearrange("p (c i t) -> p c t i", i=run, t=4)
            src = w_raw[a][:, :, h * HC:h * HC + cols].rearrange("p t (c i) -> p c t i", i=run)
            if (a, h) in V_UNITS:
                nc.vector.tensor_copy(out=dst, in_=src)
            else:
                nc.scalar.copy(out=dst, in_=src)

        def qx(a):
            nc.vector.quantize_mx(out=xc[:, a * NB:(a + 1) * NB].bitcast(FP8X4), scales=xs[:, a * NB:(a + 1) * NB],
                                  in_=xg[a][:])

        def regroup_g(a):
            gg[a] = keep.tile([P, P * 4], BF16, name="gg", align_bytes=64)
            nc.gpsimd.tensor_scalar(out=gg[a][:].rearrange("p (c t) -> p c t", t=4),
                                    in0=w_raw[a][:, :, C - P:C].rearrange("p t c -> p c t"),
                                    scalar1=1.0, scalar2=0.0, op0=ALU.mult, op1=ALU.add)

        def qw(a, h):
            lo = a * C + h * HC
            if h == 1 and a in G_SET:
                nc.vector.quantize_mx(out=wc[:, lo + P:lo + HC].bitcast(FP8X4), scales=ws[:, lo + P:lo + HC], in_=gg[a][:])
                nc.vector.quantize_mx(out=wc[:, lo:lo + P].bitcast(FP8X4), scales=ws[:, lo:lo + P], in_=wg[a, h][:])
            else:
                nc.vector.quantize_mx(out=wc[:, lo:lo + HC].bitcast(FP8X4), scales=ws[:, lo:lo + HC], in_=wg[a, h][:])

        def mm(a, h):
            pm[a, h] = psum.tile([P, 2, NB], F32, name="pm%d" % ((2 * a + h) % 4))
            for jj in range(2):
                lo = a * C + h * HC + jj * P
                nc.tensor.matmul_mx(
                    out=pm[a, h][:, jj, :],
                    lhsT=wc[:, lo:lo + P].bitcast(FP8X4), lhsT_scale=ws[:, lo:lo + P],
                    rhs=xc[:, a * NB:(a + 1) * NB].bitcast(FP8X4), rhs_scale=xs[:, a * NB:(a + 1) * NB],
                    start=True, stop=True)

        def s1(a, h, eng, jjs=(0, 1)):
            if (a, h) not in rl:
                rl[a, h] = keep.tile([P, 2 * NB], F32, name="rl%d" % ((2 * a + h) % 4))
            lo, hi = jjs[0] * NB, (jjs[-1] + 1) * NB
            prod = pm[a, h][:].rearrange("p j b -> p (j b)")[:, lo:hi]
            if eng == "S":
                rr = keep.tile([P, 2 * NB], F32, name="rr%d" % h)
                nc.scalar.activation(out=rr[:, lo:hi], in_=prod, func=ACT.Relu)
                nc.scalar.activation(out=rl[a, h][:, lo:hi], in_=rr[:, lo:hi], func=ACT.Copy, scale=w32[:, a:a + 1])
            else:
                nc.vector.tensor_scalar(out=rl[a, h][:, lo:hi], in0=prod, scalar1=0.0, scalar2=w32[:, a:a + 1],
                                        op0=ALU.max, op1=ALU.mult)

        def ta(a, h, jjs=(0, 1)):
            for jj in jjs:
                for bt in range(BT):
                    nc.tensor.matmul(
                        out=acc[h][:, bt, jj * P:(jj + 1) * P],
                        lhsT=rl[a, h][:, jj * NB + bt * P:jj * NB + (bt + 1) * P], rhs=ident[:],
                        is_transpose=True,
                        start=(a == 0 and jj == 0 and bt == 0), stop=(a == A - 1 and jj == 1 and bt == BT - 1))

        out_v = out.rearrange("(t p) c -> p t c", p=P)

        def finish(h, eng, bts):
            res = keep.tile([P, BT, HC], F32, name="res%d" % h)
            for bt in bts:
                part = slice(bt, bt + 1) if len(bts) > 1 else slice(0, BT)
                if eng == "S":
                    nc.scalar.copy(out=res[:, part, :], in_=acc[h][:, part, :])
                else:
                    nc.vector.tensor_copy(out=res[:, part, :], in_=acc[h][:, part, :])
                nc.sync.dma_start(out=out_v[:, part, h * HC:(h + 1) * HC], in_=res[:, part, :])

        tx(0)
        for i in range(A + 2):
            if i + 1 < A:
                tx(i + 1)
            if i < A:
                if i == 0:
                    ex(0)
                regroup(i, 0)
                regroup(i, 1)
                if i + 1 < A:
                    ex(i + 1)
            b = i - 1
            if 0 <= b < A:
                qx(b)
                for h in range(H):
                    qw(b, h)
                    mm(b, h)
            if i in G_SET:
                regroup_g(i)
            if i == 0:
                w_ps = psum.tile([P, 32], F32, name="acc0")
                nc.tensor.matmul(out=w_ps[:], lhsT=ones[:], rhs=w_row[:], start=True, stop=True)
            c = i - 2
            if c == 0:
                nc.vector.tensor_copy(out=w32[:], in_=w_ps[:, 0:A])
                for h in range(H):
                    acc.append(psum.tile([P, BT, HC], F32, name="acc%d" % h))
            if 0 <= c < A - 2:
                for h in range(H):
                    s1(c, h, "V")
                    ta(c, h)
        s1(6, 0, "S")
        ta(6, 0)
        s1(6, 1, "V", (0,))
        ta(6, 1, (0,))
        s1(7, 0, "V")
        ta(7, 0)
        s1(6, 1, "S", (1,))
        ta(6, 1, (1,))
        for jj in range(2):
            s1(7, 1, "V", (jj,))
            ta(7, 1, (jj,))
        finish(0, "S", (0,))
        finish(1, "V", (0, 1))
